import numpy as np
import ml_dtypes


def mxq(x, axis, fmt="e4m3"):
    dtype, down = {"e4m3": (ml_dtypes.float8_e4m3fn, 7), "e5m2": (ml_dtypes.float8_e5m2, 14)}[fmt]
    v = np.moveaxis(np.asarray(x, np.float32).astype(ml_dtypes.bfloat16).astype(np.float64), axis, -1)
    blocks = v.reshape(v.shape[:-1] + (-1, 32))
    amax = np.abs(blocks).max(-1, keepdims=True)
    byte = np.maximum(np.where(amax > 0, np.frexp(amax)[1] - 1 + 127, 0) - down, 1)
    scale = np.exp2(byte - 127.0)
    codes = (blocks / scale).astype(np.float32).astype(dtype).astype(np.float64)
    return np.moveaxis((codes * scale).reshape(v.shape), -1, axis)


WIDE = False


def mx_kscale(k):
    if not WIDE:
        return np.ones(k)
    levels = np.array([10, -10, 5, -5, 0])
    a = np.random.permutation(np.resize(levels, k // 512 * 4)).reshape(k // 512, 4)
    idx = np.arange(k)
    return np.exp2(a[idx // 512, idx % 128 // 32])


BF16 = ml_dtypes.bfloat16


def bf(x):
    return np.asarray(x, np.float32).astype(BF16)


def f64(x):
    return np.asarray(x).astype(np.float64)


SIZE, DIM, FDIM = 3072, 512, 2048
EPS = 1e-5


def setup_inputs():
    s = mx_kscale(DIM)
    r = np.random.uniform(0.4, 2.0, (SIZE, 1))
    g = np.random.standard_normal((SIZE, DIM))
    return {"lt_weight": bf(g * s / np.sqrt(np.sum(s * s)) * r),
            "Lambdas": bf(np.random.standard_normal((DIM, FDIM)) * 1.5 * np.sqrt(np.mean(s * s)) / s[:, None]),
            "bias": bf(np.random.uniform(0.0, 2.0 * np.pi, FDIM))}


def reference(lt_weight, Lambdas, bias):
    x = f64(lt_weight)
    norms = np.linalg.norm(x, axis=-1, keepdims=True)
    maxnorm = 1.0 - EPS
    e_all = x * np.minimum(1.0, maxnorm / np.maximum(norms, EPS))
    scale = np.sqrt(2.0) / np.sqrt(DIM)
    return scale * np.cos((mxq(e_all, 1, "e4m3") @ mxq(f64(Lambdas), 0, "e4m3")) + f64(bias))

@@ -1,0 +1,138 @@
+import math
+from contextlib import ExitStack
+
+import concourse.mybir as mybir
+from concourse.masks import make_identity
+
+F32 = mybir.dt.float32
+BF16 = mybir.dt.bfloat16
+I32 = mybir.dt.int32
+U32 = mybir.dt.uint32
+U8 = mybir.dt.uint8
+FP8X4 = mybir.dt.float8_e4m3fn_x4
+ALU = mybir.AluOpType
+ACT = mybir.ActivationFunctionType
+
+SIZE, DIM, FDIM = 3072, 512, 2048
+P = 128
+PACK = 4
+NT = SIZE // P
+NB = 512
+NCH = FDIM // NB
+EPS = 1e-5
+TWO_PI = 2.0 * math.pi
+FLOPS = 2 * SIZE * DIM * FDIM
+
+
+def tile_rff_kernel(tc, lt_weight, Lambdas, bias, out):
+    nc = tc.nc
+    x_view = lt_weight.rearrange("(p n) k -> p n k", n=NT)
+    out_view = out.rearrange("(p n) f -> p n f", n=NT)
+    lam_view = Lambdas.rearrange("(t p) f -> p t f", p=P)
+
+    with ExitStack() as ctx:
+        keep = ctx.enter_context(tc.tile_pool(name="keep", bufs=1))
+        stage = ctx.enter_context(tc.tile_pool(name="stage", bufs=2))
+        work = ctx.enter_context(tc.tile_pool(name="work", bufs=3))
+        psum_t = ctx.enter_context(tc.psum_pool(name="psum_t", bufs=2))
+        psum_m = ctx.enter_context(tc.psum_pool(name="psum_m", bufs=6))
+
+        x_sb = keep.tile([P, NT, DIM], BF16)
+        e_sb = keep.tile([P, NT, DIM], BF16)
+        lam_raw = keep.tile([P, PACK, FDIM], BF16)
+        lam_g = keep.tile([P, FDIM, PACK], BF16, align_bytes=64)
+        lam_codes = keep.tile([P, FDIM], U32, align_bytes=64)
+        lam_scales = keep.tile([P, FDIM], U8, align_bytes=64)
+        e_codes = keep.tile([P, SIZE], U32, align_bytes=64)
+        e_scales = keep.tile([P, SIZE], U8, align_bytes=64)
+        bias_bc = keep.tile([P, FDIM], BF16)
+        phase = keep.tile([P, FDIM], F32)
+        ident = keep.tile([P, P], BF16)
+        warm = keep.tile([P, 1], F32)
+        n2 = keep.tile([P, NT], F32)
+        nrm = keep.tile([P, NT], F32)
+        rcp = keep.tile([P, NT], F32)
+        fac = keep.tile([P, NT], F32)
+
+        xg = NT // 4
+        half = FDIM // 2
+        for g in (0, 1):
+            nc.sync.dma_start(out=x_sb[:, g * xg:(g + 1) * xg, :], in_=x_view[:, g * xg:(g + 1) * xg, :])
+        for h in (0, 1):
+            nc.sync.dma_start(out=lam_raw[:, :, h * half:(h + 1) * half], in_=lam_view[:, :, h * half:(h + 1) * half])
+        for g in (2, 3):
+            nc.sync.dma_start(out=x_sb[:, g * xg:(g + 1) * xg, :], in_=x_view[:, g * xg:(g + 1) * xg, :])
+        nc.sync.dma_start(out=bias_bc[:], in_=bias.partition_broadcast(P))
+
+        nc.vector.memset(warm[:], 1.0)
+        nc.scalar.activation(out=warm[:], in_=warm[:], func=ACT.Sqrt)
+        make_identity(nc, ident[:])
+
+        for n in range(NT):
+            junk = stage.tile([P, DIM], BF16)
+            nc.scalar.activation(out=junk[:], in_=x_sb[:, n, :], func=ACT.Square, accum_out=n2[:, n:n + 1])
+
+        for c in range(NCH):
+            cols = slice(c * NB, (c + 1) * NB)
+            nc.vector.tensor_copy(
+                out=lam_g[:, cols, :].rearrange("p (c i) t -> p c t i", i=4),
+                in_=lam_raw[:, :, cols].rearrange("p t (c i) -> p c t i", i=4),
+            )
+        for c in range(NCH):
+            cols = slice(c * NB, (c + 1) * NB)
+            nc.vector.quantize_mx(
+                out=lam_codes[:, cols].bitcast(FP8X4),
+                scales=lam_scales[:, cols],
+                in_=lam_g[:, cols, :].rearrange("p c t -> p (c t)"),
+            )
+
+        nc.vector.tensor_scalar(out=phase[:], in0=bias_bc[:], scalar1=0.5 * math.pi, scalar2=1.0 / TWO_PI,
+                                op0=ALU.add, op1=ALU.mult)
+
+        nc.scalar.activation(out=nrm[:], in_=n2[:], func=ACT.Sqrt)
+        nc.vector.tensor_scalar_max(out=nrm[:], in0=nrm[:], scalar1=EPS)
+        nc.vector.reciprocal(out=rcp[:], in_=nrm[:])
+        nc.vector.tensor_scalar(out=fac[:], in0=rcp[:], scalar1=1.0 - EPS, scalar2=1.0, op0=ALU.mult, op1=ALU.min)
+
+        for q in range(NT // 4):
+            grouped = stage.tile([P, 4, P, PACK], BF16, align_bytes=64)
+            for h in range(2):
+                xt = psum_t.tile([P, 2, PACK, P], BF16)
+                for m in range(2):
+                    n = 4 * q + 2 * h + m
+                    nc.vector.tensor_scalar(out=e_sb[:, n, :], in0=x_sb[:, n, :], scalar1=fac[:, n:n + 1],
+                                            scalar2=None, op0=ALU.mult)
+                    for t in range(PACK):
+                        nc.tensor.transpose(xt[:, m, t, :], e_sb[:, n, t * P:(t + 1) * P], ident[:])
+                nc.scalar.copy(out=grouped[:, 2 * h:2 * h + 2, :, :], in_=xt[:].rearrange("p m t r -> p m r t"))
+            cols = slice(q * NB, (q + 1) * NB)
+            nc.vector.quantize_mx(
+                out=e_codes[:, cols].bitcast(FP8X4),
+                scales=e_scales[:, cols],
+                in_=grouped[:].rearrange("p m r t -> p (m r t)"),
+            )
+
+        for n in range(NT):
+            rows = slice(n * P, (n + 1) * P)
+            turns = work.tile([P, FDIM], F32)
+            for c in range(NCH):
+                cols = slice(c * NB, (c + 1) * NB)
+                acc = psum_m.tile([P, NB], F32)
+                nc.tensor.matmul_mx(
+                    out=acc[:],
+                    lhsT=e_codes[:, rows].bitcast(FP8X4),
+                    lhsT_scale=e_scales[:, rows],
+                    rhs=lam_codes[:, cols].bitcast(FP8X4),
+                    rhs_scale=lam_scales[:, cols],
+                    start=True,
+                    stop=True,
+                )
+                nc.vector.scalar_tensor_tensor(out=turns[:, cols], in0=acc[:], scalar=1.0 / TWO_PI, in1=phase[:, cols],
+                                               op0=ALU.mult, op1=ALU.add)
+            whole = work.tile([P, FDIM], I32)
+            nc.vector.tensor_copy(out=whole[:], in_=turns[:])
+            nc.vector.tensor_tensor(out=turns[:], in0=turns[:], in1=whole[:], op=ALU.subtract)
+            res = work.tile([P, FDIM], F32)
+            nc.scalar.activation(out=res[:], in_=turns[:], func=ACT.Sin, scale=TWO_PI)
+            nc.scalar.activation(out=res[:], in_=res[:], func=ACT.Copy, scale=0.0625)
+            nc.sync.dma_start(out=out_view[:, n, :], in_=res[:])

@@ -24,6 +24,10 @@ TWO_PI = 2.0 * math.pi
 FLOPS = 2 * SIZE * DIM * FDIM
 
 
+A_ON_VECTOR = ((1, 1, 1, 1), (1, 1, 1, 1), (1, 1, 1, 1), (1, 1, 1, 1), (0, 0, 0, 1), (0, 0, 0, 1), (0, 0, 0, 1), (0, 0, 0, 1), (0, 0, 0, 1), (0, 0, 0, 1), (0, 0, 0, 1), (0, 0, 0, 1), (0, 0, 0, 1), (0, 0, 0, 1), (0, 0, 0, 1), (0, 0, 0, 1), (0, 0, 0, 1), (0, 0, 0, 1), (0, 0, 0, 1), (0, 0, 0, 1), (0, 0, 0, 1), (0, 0, 0, 1), (0, 0, 0, 1), (0, 0, 0, 1))
+TWO_TRANSPOSES = (1, 1, 1, 1, 1, 1, 1, 1, 1, 1, 1, 1, 1, 1, 1, 1, 1, 1, 1, 1, 1, 1, 1, 1)
+
+
 def tile_rff_kernel(tc, lt_weight, Lambdas, bias, out):
     nc = tc.nc
     x_view = lt_weight.rearrange("(p n) k -> p n k", n=NT)
@@ -34,8 +38,8 @@ def tile_rff_kernel(tc, lt_weight, Lambdas, bias, out):
         keep = ctx.enter_context(tc.tile_pool(name="keep", bufs=1))
         stage = ctx.enter_context(tc.tile_pool(name="stage", bufs=2))
         work = ctx.enter_context(tc.tile_pool(name="work", bufs=3))
-        psum_t = ctx.enter_context(tc.psum_pool(name="psum_t", bufs=2))
-        psum_m = ctx.enter_context(tc.psum_pool(name="psum_m", bufs=6))
+        psum_a = ctx.enter_context(tc.psum_pool(name="psum_a", bufs=4))
+        psum_b = ctx.enter_context(tc.psum_pool(name="psum_b", bufs=4))
 
         x_sb = keep.tile([P, NT, DIM], BF16)
         e_sb = keep.tile([P, NT, DIM], BF16)
@@ -45,32 +49,61 @@ def tile_rff_kernel(tc, lt_weight, Lambdas, bias, out):
         lam_scales = keep.tile([P, FDIM], U8, align_bytes=64)
         e_codes = keep.tile([P, SIZE], U32, align_bytes=64)
         e_scales = keep.tile([P, SIZE], U8, align_bytes=64)
-        bias_bc = keep.tile([P, FDIM], BF16)
-        phase = keep.tile([P, FDIM], F32)
+        bias_rows = keep.tile([P, P], BF16)
+        phase = keep.tile([P, FDIM // P], F32)
         ident = keep.tile([P, P], BF16)
+        ident_f = keep.tile([P, P], F32)
         warm = keep.tile([P, 1], F32)
         n2 = keep.tile([P, NT], F32)
         nrm = keep.tile([P, NT], F32)
+        floor = keep.tile([P, NT], F32)
         rcp = keep.tile([P, NT], F32)
         fac = keep.tile([P, NT], F32)
 
-        xg = NT // 4
         half = FDIM // 2
-        for g in (0, 1):
-            nc.sync.dma_start(out=x_sb[:, g * xg:(g + 1) * xg, :], in_=x_view[:, g * xg:(g + 1) * xg, :])
+        nc.sync.dma_start(out=x_sb[:, 0:4, :], in_=x_view[:, 0:4, :])
         for h in (0, 1):
             nc.sync.dma_start(out=lam_raw[:, :, h * half:(h + 1) * half], in_=lam_view[:, :, h * half:(h + 1) * half])
-        for g in (2, 3):
-            nc.sync.dma_start(out=x_sb[:, g * xg:(g + 1) * xg, :], in_=x_view[:, g * xg:(g + 1) * xg, :])
-        nc.sync.dma_start(out=bias_bc[:], in_=bias.partition_broadcast(P))
+        nc.vector.memset(bias_rows[:], 0.0)
+        nc.sync.dma_start(out=bias_rows[0:FDIM // P, :], in_=bias.rearrange("(a b) -> a b", b=P))
+        for g in (4, 9, 14, 19):
+            nc.sync.dma_start(out=x_sb[:, g:g + 5, :], in_=x_view[:, g:g + 5, :])
 
         nc.vector.memset(warm[:], 1.0)
         nc.scalar.activation(out=warm[:], in_=warm[:], func=ACT.Sqrt)
         make_identity(nc, ident[:])
+        make_identity(nc, ident_f[:])
 
-        for n in range(NT):
-            junk = stage.tile([P, DIM], BF16)
-            nc.scalar.activation(out=junk[:], in_=x_sb[:, n, :], func=ACT.Square, accum_out=n2[:, n:n + 1])
+        def clip_factor(lo, hi):
+            for n in range(lo, hi):
+                junk = stage.tile([P, DIM], BF16)
+                nc.scalar.activation(out=junk[:], in_=x_sb[:, n, :], func=ACT.Square, accum_out=n2[:, n:n + 1])
+            nc.scalar.activation(out=nrm[:, lo:hi], in_=n2[:, lo:hi], func=ACT.Sqrt)
+            nc.vector.tensor_scalar_max(out=floor[:, lo:hi], in0=nrm[:, lo:hi], scalar1=EPS)
+            nc.vector.reciprocal(out=rcp[:, lo:hi], in_=floor[:, lo:hi])
+            nc.vector.tensor_scalar(out=fac[:, lo:hi], in0=rcp[:, lo:hi], scalar1=1.0 - EPS, scalar2=1.0,
+                                    op0=ALU.mult, op1=ALU.min)
+
+        def front(q):
+            grouped = stage.tile([P, 4, P, PACK], BF16, align_bytes=64)
+            for h in range(2):
+                xt = psum_a.tile([P, 2, PACK, P], BF16, tag="mm")
+                for m in range(2):
+                    n = 4 * q + 2 * h + m
+                    nc.vector.tensor_scalar(out=e_sb[:, n, :], in0=x_sb[:, n, :], scalar1=fac[:, n:n + 1],
+                                            scalar2=None, op0=ALU.mult)
+                    for t in range(PACK):
+                        nc.tensor.transpose(xt[:, m, t, :], e_sb[:, n, t * P:(t + 1) * P], ident[:])
+                nc.vector.tensor_copy(out=grouped[:, 2 * h:2 * h + 2, :, :], in_=xt[:].rearrange("p m t r -> p m r t"))
+            cols = slice(q * NB, (q + 1) * NB)
+            nc.vector.quantize_mx(
+                out=e_codes[:, cols].bitcast(FP8X4),
+                scales=e_scales[:, cols],
+                in_=grouped[:].rearrange("p m r t -> p (m r t)"),
+            )
+
+        clip_factor(0, 4)
+        clip_factor(4, NT)
 
         for c in range(NCH):
             cols = slice(c * NB, (c + 1) * NB)
@@ -86,53 +119,60 @@ def tile_rff_kernel(tc, lt_weight, Lambdas, bias, out):
                 in_=lam_g[:, cols, :].rearrange("p c t -> p (c t)"),
             )
 
-        nc.vector.tensor_scalar(out=phase[:], in0=bias_bc[:], scalar1=0.5 * math.pi, scalar2=1.0 / TWO_PI,
+        bias_t = psum_b.tile([P, P], BF16, tag="tr")
+        nc.tensor.transpose(bias_t[:], bias_rows[:], ident[:])
+        nc.vector.tensor_scalar(out=phase[:], in0=bias_t[:, 0:FDIM // P], scalar1=0.5 * math.pi, scalar2=1.0 / TWO_PI,
                                 op0=ALU.add, op1=ALU.mult)
 
-        nc.scalar.activation(out=nrm[:], in_=n2[:], func=ACT.Sqrt)
-        nc.vector.tensor_scalar_max(out=nrm[:], in0=nrm[:], scalar1=EPS)
-        nc.vector.reciprocal(out=rcp[:], in_=nrm[:])
-        nc.vector.tensor_scalar(out=fac[:], in0=rcp[:], scalar1=1.0 - EPS, scalar2=1.0, op0=ALU.mult, op1=ALU.min)
+        front(0)
 
-        for q in range(NT // 4):
-            grouped = stage.tile([P, 4, P, PACK], BF16, align_bytes=64)
-            for h in range(2):
-                xt = psum_t.tile([P, 2, PACK, P], BF16)
-                for m in range(2):
-                    n = 4 * q + 2 * h + m
-                    nc.vector.tensor_scalar(out=e_sb[:, n, :], in0=x_sb[:, n, :], scalar1=fac[:, n:n + 1],
-                                            scalar2=None, op0=ALU.mult)
-                    for t in range(PACK):
-                        nc.tensor.transpose(xt[:, m, t, :], e_sb[:, n, t * P:(t + 1) * P], ident[:])
-                nc.scalar.copy(out=grouped[:, 2 * h:2 * h + 2, :, :], in_=xt[:].rearrange("p m t r -> p m r t"))
-            cols = slice(q * NB, (q + 1) * NB)
-            nc.vector.quantize_mx(
-                out=e_codes[:, cols].bitcast(FP8X4),
-                scales=e_scales[:, cols],
-                in_=grouped[:].rearrange("p m r t -> p (m r t)"),
-            )
+        for c in range(SIZE // NB):
+            ecols = slice(c * NB, (c + 1) * NB)
+            for jq in range(NCH):
+                u = c * NCH + jq
+                turns = work.tile([P, 4, NB], F32)
+                for m in range(4):
+                    jb = 4 * jq + m
+                    fcols = slice(jb * P, (jb + 1) * P)
+                    acc = psum_a.tile([P, NB], F32, tag="mm")
+                    nc.tensor.matmul_mx(
+                        out=acc[:],
+                        lhsT=lam_codes[:, fcols].bitcast(FP8X4),
+                        lhsT_scale=lam_scales[:, fcols],
+                        rhs=e_codes[:, ecols].bitcast(FP8X4),
+                        rhs_scale=e_scales[:, ecols],
+                        start=True,
+                        stop=True,
+                    )
+                    if A_ON_VECTOR[u][m]:
+                        nc.vector.tensor_scalar(out=turns[:, m, :], in0=acc[:], scalar1=1.0 / TWO_PI,
+                                                scalar2=phase[:, jb:jb + 1], op0=ALU.mult, op1=ALU.add)
+                    else:
+                        nc.scalar.activation(out=turns[:, m, :], in_=acc[:], func=ACT.Identity, scale=1.0 / TWO_PI,
+                                             bias=phase[:, jb:jb + 1])
+                whole = work.tile([P, 4, NB], I32)
+                res = work.tile([P, 4, NB], F32)
+                if TWO_TRANSPOSES[u]:
+                    nc.vector.tensor_scalar(out=whole[:], in0=turns[:], scalar1=-1.0, scalar2=None, op0=ALU.mult)
+                    minus = work.tile([P, 4, NB], F32)
+                    nc.vector.tensor_copy(out=minus[:], in_=whole[:])
+                else:
+                    nc.vector.tensor_copy(out=whole[:], in_=turns[:])
+                    nc.vector.tensor_tensor(out=turns[:], in0=turns[:], in1=whole[:], op=ALU.subtract)
+                for s in range(4):
+                    back = psum_b.tile([P, NB], F32, tag="tr")
+                    for m in range(4):
+                        if TWO_TRANSPOSES[u]:
+                            nc.tensor.matmul(out=back[:, m * P:(m + 1) * P], lhsT=turns[:, m, s * P:(s + 1) * P],
+                                             rhs=ident_f[:], is_transpose=True, start=True, stop=False)
+                            nc.tensor.matmul(out=back[:, m * P:(m + 1) * P], lhsT=minus[:, m, s * P:(s + 1) * P],
+                                             rhs=ident_f[:], is_transpose=True, start=False, stop=True)
+                        else:
+                            nc.tensor.transpose(back[:, m * P:(m + 1) * P], turns[:, m, s * P:(s + 1) * P], ident_f[:])
+                    nc.scalar.activation(out=res[:, s, :], in_=back[:], func=ACT.Sin, scale=TWO_PI)
+                    nc.gpsimd.tensor_scalar(out=res[:, s, :], in0=res[:, s, :], scalar1=0.0625, scalar2=0.0,
+                                            op0=ALU.mult, op1=ALU.add)
 
-        for n in range(NT):
-            rows = slice(n * P, (n + 1) * P)
-            turns = work.tile([P, FDIM], F32)
-            for c in range(NCH):
-                cols = slice(c * NB, (c + 1) * NB)
-                acc = psum_m.tile([P, NB], F32)
-                nc.tensor.matmul_mx(
-                    out=acc[:],
-                    lhsT=e_codes[:, rows].bitcast(FP8X4),
-                    lhsT_scale=e_scales[:, rows],
-                    rhs=lam_codes[:, cols].bitcast(FP8X4),
-                    rhs_scale=lam_scales[:, cols],
-                    start=True,
-                    stop=True,
-                )
-                nc.vector.scalar_tensor_tensor(out=turns[:, cols], in0=acc[:], scalar=1.0 / TWO_PI, in1=phase[:, cols],
-                                               op0=ALU.mult, op1=ALU.add)
-            whole = work.tile([P, FDIM], I32)
-            nc.vector.tensor_copy(out=whole[:], in_=turns[:])
-            nc.vector.tensor_tensor(out=turns[:], in0=turns[:], in1=whole[:], op=ALU.subtract)
-            res = work.tile([P, FDIM], F32)
-            nc.scalar.activation(out=res[:], in_=turns[:], func=ACT.Sin, scale=TWO_PI)
-            nc.scalar.activation(out=res[:], in_=res[:], func=ACT.Copy, scale=0.0625)
-            nc.sync.dma_start(out=out_view[:, n, :], in_=res[:])
+                nc.sync.dma_start(out=out_view[:, 4 * c:4 * c + 4, jq * NB:(jq + 1) * NB], in_=res[:])
+                if jq == 0 and c + 1 < SIZE // NB:
+                    front(c + 1)

@@ -24,8 +24,9 @@ TWO_PI = 2.0 * math.pi
 FLOPS = 2 * SIZE * DIM * FDIM
 
 
-A_ON_VECTOR = ((1, 1, 1, 1), (1, 1, 1, 1), (1, 1, 1, 1), (1, 1, 1, 1), (0, 0, 0, 1), (0, 0, 0, 1), (0, 0, 0, 1), (0, 0, 0, 1), (0, 0, 0, 1), (0, 0, 0, 1), (0, 0, 0, 1), (0, 0, 0, 1), (0, 0, 0, 1), (0, 0, 0, 1), (0, 0, 0, 1), (0, 0, 0, 1), (0, 0, 0, 1), (0, 0, 0, 1), (0, 0, 0, 1), (0, 0, 0, 1), (0, 0, 0, 1), (0, 0, 0, 1), (0, 0, 0, 1), (0, 0, 0, 1))
-TWO_TRANSPOSES = (1, 1, 1, 1, 1, 1, 1, 1, 1, 1, 1, 1, 1, 1, 1, 1, 1, 1, 1, 1, 1, 1, 1, 1)
+A_ON_VECTOR = ((1, 1, 1, 1), (1, 1, 1, 1), (1, 1, 1, 1), (0, 0, 0, 1), (0, 0, 0, 0), (0, 0, 0, 0), (0, 0, 0, 0), (0, 0, 0, 0), (0, 0, 0, 0), (0, 0, 0, 0), (0, 0, 0, 1), (0, 0, 0, 0), (0, 0, 0, 0), (0, 0, 0, 0), (0, 0, 0, 0), (0, 0, 0, 0), (0, 0, 0, 0), (0, 0, 0, 1), (0, 0, 0, 0), (0, 0, 0, 0), (0, 0, 0, 0), (0, 0, 0, 0), (0, 0, 0, 0), (0, 0, 0, 0))
+E_ENGINE = ("pool", "pool", "pool", "pool", "pool", "pool", "pool", "pool", "pool", "pool", "pool", "pool", "pool", "pool", "pool", "pool", "pool", "pool", "pool", "pool", "pool", "pool", "pool", "pool")
+TWO_TRANSPOSES = (0, 0, 0, 0, 0, 0, 0, 0, 0, 0, 0, 0, 0, 0, 0, 0, 0, 0, 0, 0, 0, 0, 0, 0)
 
 
 def tile_rff_kernel(tc, lt_weight, Lambdas, bias, out):
@@ -38,6 +39,8 @@ def tile_rff_kernel(tc, lt_weight, Lambdas, bias, out):
         keep = ctx.enter_context(tc.tile_pool(name="keep", bufs=1))
         stage = ctx.enter_context(tc.tile_pool(name="stage", bufs=2))
         work = ctx.enter_context(tc.tile_pool(name="work", bufs=3))
+        bank = ctx.enter_context(tc.tile_pool(name="bank", bufs=14))
+        ints = ctx.enter_context(tc.tile_pool(name="ints", bufs=3))
         psum_a = ctx.enter_context(tc.psum_pool(name="psum_a", bufs=4))
         psum_b = ctx.enter_context(tc.psum_pool(name="psum_b", bufs=4))
 
@@ -61,12 +64,13 @@ def tile_rff_kernel(tc, lt_weight, Lambdas, bias, out):
         fac = keep.tile([P, NT], F32)
 
         half = FDIM // 2
-        nc.sync.dma_start(out=x_sb[:, 0:4, :], in_=x_view[:, 0:4, :])
-        for h in (0, 1):
-            nc.sync.dma_start(out=lam_raw[:, :, h * half:(h + 1) * half], in_=lam_view[:, :, h * half:(h + 1) * half])
         nc.vector.memset(bias_rows[:], 0.0)
+        nc.sync.dma_start(out=x_sb[:, 0:4, :], in_=x_view[:, 0:4, :])
+        nc.sync.dma_start(out=lam_raw[:, :, 0:half], in_=lam_view[:, :, 0:half])
+        nc.sync.dma_start(out=x_sb[:, 4:9, :], in_=x_view[:, 4:9, :])
+        nc.sync.dma_start(out=lam_raw[:, :, half:FDIM], in_=lam_view[:, :, half:FDIM])
         nc.sync.dma_start(out=bias_rows[0:FDIM // P, :], in_=bias.rearrange("(a b) -> a b", b=P))
-        for g in (4, 9, 14, 19):
+        for g in (9, 14, 19):
             nc.sync.dma_start(out=x_sb[:, g:g + 5, :], in_=x_view[:, g:g + 5, :])
 
         nc.vector.memset(warm[:], 1.0)
@@ -130,7 +134,7 @@ def tile_rff_kernel(tc, lt_weight, Lambdas, bias, out):
             ecols = slice(c * NB, (c + 1) * NB)
             for jq in range(NCH):
                 u = c * NCH + jq
-                turns = work.tile([P, 4, NB], F32)
+                res = work.tile([P, 4, NB], F32)
                 for m in range(4):
                     jb = 4 * jq + m
                     fcols = slice(jb * P, (jb + 1) * P)
@@ -144,35 +148,39 @@ def tile_rff_kernel(tc, lt_weight, Lambdas, bias, out):
                         start=True,
                         stop=True,
                     )
+                    turns = bank.tile([P, NB], F32)
                     if A_ON_VECTOR[u][m]:
-                        nc.vector.tensor_scalar(out=turns[:, m, :], in0=acc[:], scalar1=1.0 / TWO_PI,
+                        nc.vector.tensor_scalar(out=turns[:], in0=acc[:], scalar1=1.0 / TWO_PI,
                                                 scalar2=phase[:, jb:jb + 1], op0=ALU.mult, op1=ALU.add)
                     else:
-                        nc.scalar.activation(out=turns[:, m, :], in_=acc[:], func=ACT.Identity, scale=1.0 / TWO_PI,
+                        nc.scalar.activation(out=turns[:], in_=acc[:], func=ACT.Identity, scale=1.0 / TWO_PI,
                                              bias=phase[:, jb:jb + 1])
-                whole = work.tile([P, 4, NB], I32)
-                res = work.tile([P, 4, NB], F32)
-                if TWO_TRANSPOSES[u]:
-                    nc.vector.tensor_scalar(out=whole[:], in0=turns[:], scalar1=-1.0, scalar2=None, op0=ALU.mult)
-                    minus = work.tile([P, 4, NB], F32)
-                    nc.vector.tensor_copy(out=minus[:], in_=whole[:])
-                else:
-                    nc.vector.tensor_copy(out=whole[:], in_=turns[:])
-                    nc.vector.tensor_tensor(out=turns[:], in0=turns[:], in1=whole[:], op=ALU.subtract)
-                for s in range(4):
+                    whole = ints.tile([P, NB], I32)
                     back = psum_b.tile([P, NB], F32, tag="tr")
-                    for m in range(4):
-                        if TWO_TRANSPOSES[u]:
-                            nc.tensor.matmul(out=back[:, m * P:(m + 1) * P], lhsT=turns[:, m, s * P:(s + 1) * P],
-                                             rhs=ident_f[:], is_transpose=True, start=True, stop=False)
-                            nc.tensor.matmul(out=back[:, m * P:(m + 1) * P], lhsT=minus[:, m, s * P:(s + 1) * P],
-                                             rhs=ident_f[:], is_transpose=True, start=False, stop=True)
-                        else:
-                            nc.tensor.transpose(back[:, m * P:(m + 1) * P], turns[:, m, s * P:(s + 1) * P], ident_f[:])
-                    nc.scalar.activation(out=res[:, s, :], in_=back[:], func=ACT.Sin, scale=TWO_PI)
-                    nc.gpsimd.tensor_scalar(out=res[:, s, :], in0=res[:, s, :], scalar1=0.0625, scalar2=0.0,
-                                            op0=ALU.mult, op1=ALU.add)
-
+                    if TWO_TRANSPOSES[u]:
+                        nc.vector.tensor_scalar(out=whole[:], in0=turns[:], scalar1=-1.0, scalar2=None, op0=ALU.mult)
+                        minus = bank.tile([P, NB], F32)
+                        nc.vector.tensor_copy(out=minus[:], in_=whole[:])
+                        for s in range(4):
+                            blk = slice(s * P, (s + 1) * P)
+                            nc.tensor.matmul(out=back[:, blk], lhsT=turns[:, blk], rhs=ident_f[:], is_transpose=True,
+                                             start=True, stop=False)
+                            nc.tensor.matmul(out=back[:, blk], lhsT=minus[:, blk], rhs=ident_f[:], is_transpose=True,
+                                             start=False, stop=True)
+                    else:
+                        nc.vector.tensor_copy(out=whole[:], in_=turns[:])
+                        nc.vector.tensor_tensor(out=turns[:], in0=turns[:], in1=whole[:], op=ALU.subtract)
+                        for s in range(4):
+                            blk = slice(s * P, (s + 1) * P)
+                            nc.tensor.transpose(back[:, blk], turns[:, blk], ident_f[:])
+                    nc.scalar.activation(out=res[:, :, m * P:(m + 1) * P], in_=back[:].rearrange("p (s j) -> p s j", s=4),
+                                         func=ACT.Sin, scale=TWO_PI)
+                if E_ENGINE[u] == "pool":
+                    nc.gpsimd.tensor_scalar(out=res[:], in0=res[:], scalar1=0.0625, scalar2=0.0, op0=ALU.mult, op1=ALU.add)
+                elif E_ENGINE[u] == "act":
+                    nc.scalar.activation(out=res[:], in_=res[:], func=ACT.Copy, scale=0.0625)
+                else:
+                    nc.vector.tensor_scalar(out=res[:], in0=res[:], scalar1=0.0625, scalar2=None, op0=ALU.mult)
                 nc.sync.dma_start(out=out_view[:, 4 * c:4 * c + 4, jq * NB:(jq + 1) * NB], in_=res[:])
                 if jq == 0 and c + 1 < SIZE // NB:
                     front(c + 1)

@@ -24,9 +24,8 @@ TWO_PI = 2.0 * math.pi
 FLOPS = 2 * SIZE * DIM * FDIM
 
 
-A_ON_VECTOR = ((1, 1, 1, 1), (1, 1, 1, 1), (1, 1, 1, 1), (0, 0, 0, 1), (0, 0, 0, 0), (0, 0, 0, 0), (0, 0, 0, 0), (0, 0, 0, 0), (0, 0, 0, 0), (0, 0, 0, 0), (0, 0, 0, 1), (0, 0, 0, 0), (0, 0, 0, 0), (0, 0, 0, 0), (0, 0, 0, 0), (0, 0, 0, 0), (0, 0, 0, 0), (0, 0, 0, 1), (0, 0, 0, 0), (0, 0, 0, 0), (0, 0, 0, 0), (0, 0, 0, 0), (0, 0, 0, 0), (0, 0, 0, 0))
-E_ENGINE = ("pool", "pool", "pool", "pool", "pool", "pool", "pool", "pool", "pool", "pool", "pool", "pool", "pool", "pool", "pool", "pool", "pool", "pool", "pool", "pool", "pool", "pool", "pool", "pool")
-TWO_TRANSPOSES = (0, 0, 0, 0, 0, 0, 0, 0, 0, 0, 0, 0, 0, 0, 0, 0, 0, 0, 0, 0, 0, 0, 0, 0)
+A_ON_VECTOR = ((1, 1, 1, 1), (1, 1, 1, 1), (1, 1, 1, 1), (0, 0, 0, 0), (0, 0, 0, 0), (0, 0, 0, 1), (0, 0, 0, 0), (0, 0, 0, 0), (0, 0, 0, 0), (0, 0, 0, 0), (0, 0, 0, 0), (0, 0, 0, 0), (0, 0, 0, 0), (0, 0, 0, 0), (0, 0, 0, 0), (0, 0, 0, 1), (0, 0, 0, 0), (0, 0, 0, 0), (0, 0, 0, 0), (0, 0, 0, 0), (0, 0, 0, 0), (0, 0, 0, 0), (0, 0, 0, 0), (0, 0, 0, 0))
+TWO_TRANSPOSES = (1, 1, 1, 1, 1, 1, 1, 1, 1, 1, 1, 1, 1, 1, 1, 1, 1, 1, 1, 1, 1, 1, 1, 1)
 
 
 def tile_rff_kernel(tc, lt_weight, Lambdas, bias, out):
@@ -39,8 +38,6 @@ def tile_rff_kernel(tc, lt_weight, Lambdas, bias, out):
         keep = ctx.enter_context(tc.tile_pool(name="keep", bufs=1))
         stage = ctx.enter_context(tc.tile_pool(name="stage", bufs=2))
         work = ctx.enter_context(tc.tile_pool(name="work", bufs=3))
-        bank = ctx.enter_context(tc.tile_pool(name="bank", bufs=14))
-        ints = ctx.enter_context(tc.tile_pool(name="ints", bufs=3))
         psum_a = ctx.enter_context(tc.psum_pool(name="psum_a", bufs=4))
         psum_b = ctx.enter_context(tc.psum_pool(name="psum_b", bufs=4))
 
@@ -64,13 +61,12 @@ def tile_rff_kernel(tc, lt_weight, Lambdas, bias, out):
         fac = keep.tile([P, NT], F32)
 
         half = FDIM // 2
-        nc.vector.memset(bias_rows[:], 0.0)
         nc.sync.dma_start(out=x_sb[:, 0:4, :], in_=x_view[:, 0:4, :])
-        nc.sync.dma_start(out=lam_raw[:, :, 0:half], in_=lam_view[:, :, 0:half])
-        nc.sync.dma_start(out=x_sb[:, 4:9, :], in_=x_view[:, 4:9, :])
-        nc.sync.dma_start(out=lam_raw[:, :, half:FDIM], in_=lam_view[:, :, half:FDIM])
+        for h in (0, 1):
+            nc.sync.dma_start(out=lam_raw[:, :, h * half:(h + 1) * half], in_=lam_view[:, :, h * half:(h + 1) * half])
+        nc.vector.memset(bias_rows[:], 0.0)
         nc.sync.dma_start(out=bias_rows[0:FDIM // P, :], in_=bias.rearrange("(a b) -> a b", b=P))
-        for g in (9, 14, 19):
+        for g in (4, 9, 14, 19):
             nc.sync.dma_start(out=x_sb[:, g:g + 5, :], in_=x_view[:, g:g + 5, :])
 
         nc.vector.memset(warm[:], 1.0)
@@ -134,7 +130,7 @@ def tile_rff_kernel(tc, lt_weight, Lambdas, bias, out):
             ecols = slice(c * NB, (c + 1) * NB)
             for jq in range(NCH):
                 u = c * NCH + jq
-                res = work.tile([P, 4, NB], F32)
+                turns = work.tile([P, 4, NB], F32)
                 for m in range(4):
                     jb = 4 * jq + m
                     fcols = slice(jb * P, (jb + 1) * P)
@@ -148,39 +144,34 @@ def tile_rff_kernel(tc, lt_weight, Lambdas, bias, out):
                         start=True,
                         stop=True,
                     )
-                    turns = bank.tile([P, NB], F32)
                     if A_ON_VECTOR[u][m]:
-                        nc.vector.tensor_scalar(out=turns[:], in0=acc[:], scalar1=1.0 / TWO_PI,
+                        nc.vector.tensor_scalar(out=turns[:, m, :], in0=acc[:], scalar1=1.0 / TWO_PI,
                                                 scalar2=phase[:, jb:jb + 1], op0=ALU.mult, op1=ALU.add)
                     else:
-                        nc.scalar.activation(out=turns[:], in_=acc[:], func=ACT.Identity, scale=1.0 / TWO_PI,
+                        nc.scalar.activation(out=turns[:, m, :], in_=acc[:], func=ACT.Identity, scale=1.0 / TWO_PI,
                                              bias=phase[:, jb:jb + 1])
-                    whole = ints.tile([P, NB], I32)
-                    back = psum_b.tile([P, NB], F32, tag="tr")
-                    if TWO_TRANSPOSES[u]:
-                        nc.vector.tensor_scalar(out=whole[:], in0=turns[:], scalar1=-1.0, scalar2=None, op0=ALU.mult)
-                        minus = bank.tile([P, NB], F32)
-                        nc.vector.tensor_copy(out=minus[:], in_=whole[:])
-                        for s in range(4):
-                            blk = slice(s * P, (s + 1) * P)
-                            nc.tensor.matmul(out=back[:, blk], lhsT=turns[:, blk], rhs=ident_f[:], is_transpose=True,
-                                             start=True, stop=False)
-                            nc.tensor.matmul(out=back[:, blk], lhsT=minus[:, blk], rhs=ident_f[:], is_transpose=True,
-                                             start=False, stop=True)
-                    else:
-                        nc.vector.tensor_copy(out=whole[:], in_=turns[:])
-                        nc.vector.tensor_tensor(out=turns[:], in0=turns[:], in1=whole[:], op=ALU.subtract)
-                        for s in range(4):
-                            blk = slice(s * P, (s + 1) * P)
-                            nc.tensor.transpose(back[:, blk], turns[:, blk], ident_f[:])
-                    nc.scalar.activation(out=res[:, :, m * P:(m + 1) * P], in_=back[:].rearrange("p (s j) -> p s j", s=4),
-                                         func=ACT.Sin, scale=TWO_PI)
-                if E_ENGINE[u] == "pool":
-                    nc.gpsimd.tensor_scalar(out=res[:], in0=res[:], scalar1=0.0625, scalar2=0.0, op0=ALU.mult, op1=ALU.add)
-                elif E_ENGINE[u] == "act":
-                    nc.scalar.activation(out=res[:], in_=res[:], func=ACT.Copy, scale=0.0625)
+                whole = work.tile([P, 4, NB], I32)
+                res = work.tile([P, 4, NB], F32)
+                if TWO_TRANSPOSES[u]:
+                    nc.vector.tensor_scalar(out=whole[:], in0=turns[:], scalar1=-1.0, scalar2=None, op0=ALU.mult)
+                    minus = work.tile([P, 4, NB], F32)
+                    nc.vector.tensor_copy(out=minus[:], in_=whole[:])
                 else:
-                    nc.vector.tensor_scalar(out=res[:], in0=res[:], scalar1=0.0625, scalar2=None, op0=ALU.mult)
+                    nc.vector.tensor_copy(out=whole[:], in_=turns[:])
+                    nc.vector.tensor_tensor(out=turns[:], in0=turns[:], in1=whole[:], op=ALU.subtract)
+                for s in range(4):
+                    back = psum_b.tile([P, NB], F32, tag="tr")
+                    for m in range(4):
+                        if TWO_TRANSPOSES[u]:
+                            nc.tensor.matmul(out=back[:, m * P:(m + 1) * P], lhsT=turns[:, m, s * P:(s + 1) * P],
+                                             rhs=ident_f[:], is_transpose=True, start=True, stop=False)
+                            nc.tensor.matmul(out=back[:, m * P:(m + 1) * P], lhsT=minus[:, m, s * P:(s + 1) * P],
+                                             rhs=ident_f[:], is_transpose=True, start=False, stop=True)
+                        else:
+                            nc.tensor.transpose(back[:, m * P:(m + 1) * P], turns[:, m, s * P:(s + 1) * P], ident_f[:])
+                    nc.scalar.activation(out=res[:, s, :], in_=back[:], func=ACT.Sin, scale=TWO_PI)
+
+                nc.vector.tensor_scalar(out=res[:], in0=res[:], scalar1=0.0625, scalar2=None, op0=ALU.mult)
                 nc.sync.dma_start(out=out_view[:, 4 * c:4 * c + 4, jq * NB:(jq + 1) * NB], in_=res[:])
                 if jq == 0 and c + 1 < SIZE // NB:
                     front(c + 1)

@@ -24,8 +24,16 @@ TWO_PI = 2.0 * math.pi
 FLOPS = 2 * SIZE * DIM * FDIM
 
 
-A_ON_VECTOR = ((1, 1, 1, 1), (1, 1, 1, 1), (1, 1, 1, 1), (0, 0, 0, 0), (0, 0, 0, 0), (0, 0, 0, 1), (0, 0, 0, 0), (0, 0, 0, 0), (0, 0, 0, 0), (0, 0, 0, 0), (0, 0, 0, 0), (0, 0, 0, 0), (0, 0, 0, 0), (0, 0, 0, 0), (0, 0, 0, 0), (0, 0, 0, 1), (0, 0, 0, 0), (0, 0, 0, 0), (0, 0, 0, 0), (0, 0, 0, 0), (0, 0, 0, 0), (0, 0, 0, 0), (0, 0, 0, 0), (0, 0, 0, 0))
-TWO_TRANSPOSES = (1, 1, 1, 1, 1, 1, 1, 1, 1, 1, 1, 1, 1, 1, 1, 1, 1, 1, 1, 1, 1, 1, 1, 1)
+NBANK = (SIZE // NB) * (FDIM // P)
+NPAIR = NBANK // 2
+
+
+def on_vector(j):
+    return j % 12 == 5
+
+
+def two_transposes(j):
+    return False
 
 
 def tile_rff_kernel(tc, lt_weight, Lambdas, bias, out):
@@ -37,7 +45,10 @@ def tile_rff_kernel(tc, lt_weight, Lambdas, bias, out):
     with ExitStack() as ctx:
         keep = ctx.enter_context(tc.tile_pool(name="keep", bufs=1))
         stage = ctx.enter_context(tc.tile_pool(name="stage", bufs=2))
-        work = ctx.enter_context(tc.tile_pool(name="work", bufs=3))
+        work = ctx.enter_context(tc.tile_pool(name="work", bufs=4))
+        bank = ctx.enter_context(tc.tile_pool(name="bank", bufs=8))
+        nega = ctx.enter_context(tc.tile_pool(name="nega", bufs=6))
+        ints = ctx.enter_context(tc.tile_pool(name="ints", bufs=4))
         psum_a = ctx.enter_context(tc.psum_pool(name="psum_a", bufs=4))
         psum_b = ctx.enter_context(tc.psum_pool(name="psum_b", bufs=4))
 
@@ -61,13 +72,14 @@ def tile_rff_kernel(tc, lt_weight, Lambdas, bias, out):
         fac = keep.tile([P, NT], F32)
 
         half = FDIM // 2
-        nc.sync.dma_start(out=x_sb[:, 0:4, :], in_=x_view[:, 0:4, :])
-        for h in (0, 1):
-            nc.sync.dma_start(out=lam_raw[:, :, h * half:(h + 1) * half], in_=lam_view[:, :, h * half:(h + 1) * half])
         nc.vector.memset(bias_rows[:], 0.0)
+        nc.sync.dma_start(out=x_sb[:, 0:4, :], in_=x_view[:, 0:4, :])
+        nc.sync.dma_start(out=lam_raw[:, :, 0:half], in_=lam_view[:, :, 0:half])
+        nc.sync.dma_start(out=x_sb[:, 4:8, :], in_=x_view[:, 4:8, :])
+        nc.sync.dma_start(out=lam_raw[:, :, half:FDIM], in_=lam_view[:, :, half:FDIM])
         nc.sync.dma_start(out=bias_rows[0:FDIM // P, :], in_=bias.rearrange("(a b) -> a b", b=P))
-        for g in (4, 9, 14, 19):
-            nc.sync.dma_start(out=x_sb[:, g:g + 5, :], in_=x_view[:, g:g + 5, :])
+        for g in (8, 12, 16, 20):
+            nc.sync.dma_start(out=x_sb[:, g:g + 4, :], in_=x_view[:, g:g + 4, :])
 
         nc.vector.memset(warm[:], 1.0)
         nc.scalar.activation(out=warm[:], in_=warm[:], func=ACT.Sqrt)
@@ -94,7 +106,11 @@ def tile_rff_kernel(tc, lt_weight, Lambdas, bias, out):
                                             scalar2=None, op0=ALU.mult)
                     for t in range(PACK):
                         nc.tensor.transpose(xt[:, m, t, :], e_sb[:, n, t * P:(t + 1) * P], ident[:])
-                nc.vector.tensor_copy(out=grouped[:, 2 * h:2 * h + 2, :, :], in_=xt[:].rearrange("p m t r -> p m r t"))
+                if h == 0:
+                    nc.scalar.copy(out=grouped[:, 2 * h:2 * h + 2, :, :], in_=xt[:].rearrange("p m t r -> p m r t"))
+                else:
+                    nc.vector.tensor_copy(out=grouped[:, 2 * h:2 * h + 2, :, :],
+                                          in_=xt[:].rearrange("p m t r -> p m r t"))
             cols = slice(q * NB, (q + 1) * NB)
             nc.vector.quantize_mx(
                 out=e_codes[:, cols].bitcast(FP8X4),
@@ -102,8 +118,8 @@ def tile_rff_kernel(tc, lt_weight, Lambdas, bias, out):
                 in_=grouped[:].rearrange("p m r t -> p (m r t)"),
             )
 
-        clip_factor(0, 4)
-        clip_factor(4, NT)
+        for q in range(SIZE // NB):
+            clip_factor(4 * q, 4 * q + 4)
 
         for c in range(NCH):
             cols = slice(c * NB, (c + 1) * NB)
@@ -124,54 +140,100 @@ def tile_rff_kernel(tc, lt_weight, Lambdas, bias, out):
         nc.vector.tensor_scalar(out=phase[:], in0=bias_t[:, 0:FDIM // P], scalar1=0.5 * math.pi, scalar2=1.0 / TWO_PI,
                                 op0=ALU.add, op1=ALU.mult)
 
-        front(0)
+        for q in range(SIZE // NB):
+            front(q)
 
-        for c in range(SIZE // NB):
+        acc = {}
+        turns = {}
+        minus = {}
+        whole = {}
+        back = {}
+        res = {}
+
+        def product(j):
+            c, jb = divmod(j, FDIM // P)
+            fcols = slice(jb * P, (jb + 1) * P)
             ecols = slice(c * NB, (c + 1) * NB)
-            for jq in range(NCH):
-                u = c * NCH + jq
-                turns = work.tile([P, 4, NB], F32)
-                for m in range(4):
-                    jb = 4 * jq + m
-                    fcols = slice(jb * P, (jb + 1) * P)
-                    acc = psum_a.tile([P, NB], F32, tag="mm")
-                    nc.tensor.matmul_mx(
-                        out=acc[:],
-                        lhsT=lam_codes[:, fcols].bitcast(FP8X4),
-                        lhsT_scale=lam_scales[:, fcols],
-                        rhs=e_codes[:, ecols].bitcast(FP8X4),
-                        rhs_scale=e_scales[:, ecols],
-                        start=True,
-                        stop=True,
-                    )
-                    if A_ON_VECTOR[u][m]:
-                        nc.vector.tensor_scalar(out=turns[:, m, :], in0=acc[:], scalar1=1.0 / TWO_PI,
-                                                scalar2=phase[:, jb:jb + 1], op0=ALU.mult, op1=ALU.add)
-                    else:
-                        nc.scalar.activation(out=turns[:, m, :], in_=acc[:], func=ACT.Identity, scale=1.0 / TWO_PI,
-                                             bias=phase[:, jb:jb + 1])
-                whole = work.tile([P, 4, NB], I32)
-                res = work.tile([P, 4, NB], F32)
-                if TWO_TRANSPOSES[u]:
-                    nc.vector.tensor_scalar(out=whole[:], in0=turns[:], scalar1=-1.0, scalar2=None, op0=ALU.mult)
-                    minus = work.tile([P, 4, NB], F32)
-                    nc.vector.tensor_copy(out=minus[:], in_=whole[:])
-                else:
-                    nc.vector.tensor_copy(out=whole[:], in_=turns[:])
-                    nc.vector.tensor_tensor(out=turns[:], in0=turns[:], in1=whole[:], op=ALU.subtract)
-                for s in range(4):
-                    back = psum_b.tile([P, NB], F32, tag="tr")
-                    for m in range(4):
-                        if TWO_TRANSPOSES[u]:
-                            nc.tensor.matmul(out=back[:, m * P:(m + 1) * P], lhsT=turns[:, m, s * P:(s + 1) * P],
-                                             rhs=ident_f[:], is_transpose=True, start=True, stop=False)
-                            nc.tensor.matmul(out=back[:, m * P:(m + 1) * P], lhsT=minus[:, m, s * P:(s + 1) * P],
-                                             rhs=ident_f[:], is_transpose=True, start=False, stop=True)
-                        else:
-                            nc.tensor.transpose(back[:, m * P:(m + 1) * P], turns[:, m, s * P:(s + 1) * P], ident_f[:])
-                    nc.scalar.activation(out=res[:, s, :], in_=back[:], func=ACT.Sin, scale=TWO_PI)
+            acc[j] = psum_a.tile([P, NB], F32, name="acc", tag="mm")
+            nc.tensor.matmul_mx(
+                out=acc[j][:],
+                lhsT=lam_codes[:, fcols].bitcast(FP8X4),
+                lhsT_scale=lam_scales[:, fcols],
+                rhs=e_codes[:, ecols].bitcast(FP8X4),
+                rhs_scale=e_scales[:, ecols],
+                start=True,
+                stop=True,
+            )
 
-                nc.vector.tensor_scalar(out=res[:], in0=res[:], scalar1=0.0625, scalar2=None, op0=ALU.mult)
-                nc.sync.dma_start(out=out_view[:, 4 * c:4 * c + 4, jq * NB:(jq + 1) * NB], in_=res[:])
-                if jq == 0 and c + 1 < SIZE // NB:
-                    front(c + 1)
+        def leave(j):
+            jb = j % (FDIM // P)
+            turns[j] = bank.tile([P, NB], F32, name="turns")
+            if on_vector(j):
+                nc.vector.tensor_scalar(out=turns[j][:], in0=acc[j][:], scalar1=1.0 / TWO_PI,
+                                        scalar2=phase[:, jb:jb + 1], op0=ALU.mult, op1=ALU.add)
+            else:
+                nc.scalar.activation(out=turns[j][:], in_=acc[j][:], func=ACT.Identity, scale=1.0 / TWO_PI,
+                                     bias=phase[:, jb:jb + 1])
+
+        def whole_turns(j):
+            whole[j] = ints.tile([P, NB], I32, name="whole")
+            if two_transposes(j):
+                nc.vector.tensor_scalar(out=whole[j][:], in0=turns[j][:], scalar1=-1.0, scalar2=None, op0=ALU.mult)
+            else:
+                nc.vector.tensor_copy(out=whole[j][:], in_=turns[j][:])
+
+        def fraction(j):
+            if two_transposes(j):
+                minus[j] = nega.tile([P, NB], F32, name="minus")
+                nc.vector.tensor_copy(out=minus[j][:], in_=whole[j][:])
+            else:
+                nc.vector.tensor_tensor(out=turns[j][:], in0=turns[j][:], in1=whole[j][:], op=ALU.subtract)
+
+        def turn_back(j):
+            back[j] = psum_b.tile([P, NB], F32, name="back", tag="tr")
+            for s in range(4):
+                blk = slice(s * P, (s + 1) * P)
+                if two_transposes(j):
+                    nc.tensor.matmul(out=back[j][:, blk], lhsT=turns[j][:, blk], rhs=ident_f[:], is_transpose=True,
+                                     start=True, stop=False)
+                    nc.tensor.matmul(out=back[j][:, blk], lhsT=minus[j][:, blk], rhs=ident_f[:], is_transpose=True,
+                                     start=False, stop=True)
+                else:
+                    nc.tensor.transpose(back[j][:, blk], turns[j][:, blk], ident_f[:])
+
+        def sine(j):
+            u, m = divmod(j, 4)
+            if m == 0:
+                res[u] = work.tile([P, 4, NB], F32, name="res")
+            nc.scalar.activation(out=res[u][:, :, m * P:(m + 1) * P], in_=back[j][:].rearrange("p (s j) -> p s j", s=4),
+                                 func=ACT.Sin, scale=TWO_PI)
+
+        def finish(u):
+            c, jq = divmod(u, NCH)
+            nc.vector.tensor_scalar(out=res[u][:], in0=res[u][:], scalar1=0.0625, scalar2=None, op0=ALU.mult)
+            nc.sync.dma_start(out=out_view[:, 4 * c:4 * c + 4, jq * NB:(jq + 1) * NB], in_=res[u][:])
+
+        def pair(s):
+            return [j for j in (2 * s, 2 * s + 1) if 0 <= j < NBANK]
+
+        with tc.manual_schedule():
+            for s in range(NPAIR + 6 + 1):
+                for j in pair(s):
+                    product(j)
+                for j in pair(s - 3):
+                    turn_back(j)
+                for k in range(2):
+                    for j in pair(s - 1)[k:k + 1]:
+                        if not on_vector(j):
+                            leave(j)
+                    for j in pair(s - 4)[k:k + 1]:
+                        sine(j)
+                for j in pair(s - 2):
+                    whole_turns(j)
+                for j in pair(s - 1):
+                    if on_vector(j):
+                        leave(j)
+                if (s - 6) % 2 == 0 and 0 <= (s - 6) // 2 < NBANK // 4:
+                    finish((s - 6) // 2)
+                for j in pair(s - 2):
+                    fraction(j)

@@ -29,11 +29,11 @@ NPAIR = NBANK // 2
 
 
 def on_vector(j):
-    return j % 12 == 5
+    return j % 7 == 5
 
 
-def two_transposes(j):
-    return False
+def two_transposes(q):
+    return q % 2 == 1
 
 
 def tile_rff_kernel(tc, lt_weight, Lambdas, bias, out):
@@ -46,9 +46,9 @@ def tile_rff_kernel(tc, lt_weight, Lambdas, bias, out):
         keep = ctx.enter_context(tc.tile_pool(name="keep", bufs=1))
         stage = ctx.enter_context(tc.tile_pool(name="stage", bufs=2))
         work = ctx.enter_context(tc.tile_pool(name="work", bufs=4))
-        bank = ctx.enter_context(tc.tile_pool(name="bank", bufs=8))
-        nega = ctx.enter_context(tc.tile_pool(name="nega", bufs=6))
-        ints = ctx.enter_context(tc.tile_pool(name="ints", bufs=4))
+        bank = ctx.enter_context(tc.tile_pool(name="bank", bufs=6))
+        nega = ctx.enter_context(tc.tile_pool(name="nega", bufs=3))
+        ints = ctx.enter_context(tc.tile_pool(name="ints", bufs=3))
         psum_a = ctx.enter_context(tc.psum_pool(name="psum_a", bufs=4))
         psum_b = ctx.enter_context(tc.psum_pool(name="psum_b", bufs=4))
 
@@ -145,8 +145,8 @@ def tile_rff_kernel(tc, lt_weight, Lambdas, bias, out):
 
         acc = {}
         turns = {}
-        minus = {}
         whole = {}
+        minus = {}
         back = {}
         res = {}
 
@@ -167,39 +167,42 @@ def tile_rff_kernel(tc, lt_weight, Lambdas, bias, out):
 
         def leave(j):
             jb = j % (FDIM // P)
-            turns[j] = bank.tile([P, NB], F32, name="turns")
+            q, k = divmod(j, 2)
+            if q not in turns:
+                turns[q] = bank.tile([P, 2, NB], F32, name="turns")
             if on_vector(j):
-                nc.vector.tensor_scalar(out=turns[j][:], in0=acc[j][:], scalar1=1.0 / TWO_PI,
+                nc.vector.tensor_scalar(out=turns[q][:, k, :], in0=acc[j][:], scalar1=1.0 / TWO_PI,
                                         scalar2=phase[:, jb:jb + 1], op0=ALU.mult, op1=ALU.add)
             else:
-                nc.scalar.activation(out=turns[j][:], in_=acc[j][:], func=ACT.Identity, scale=1.0 / TWO_PI,
+                nc.scalar.activation(out=turns[q][:, k, :], in_=acc[j][:], func=ACT.Identity, scale=1.0 / TWO_PI,
                                      bias=phase[:, jb:jb + 1])
 
-        def whole_turns(j):
-            whole[j] = ints.tile([P, NB], I32, name="whole")
-            if two_transposes(j):
-                nc.vector.tensor_scalar(out=whole[j][:], in0=turns[j][:], scalar1=-1.0, scalar2=None, op0=ALU.mult)
+        def whole_turns(q):
+            whole[q] = ints.tile([P, 2, NB], I32, name="whole")
+            if two_transposes(q):
+                nc.vector.tensor_scalar(out=whole[q][:], in0=turns[q][:], scalar1=-1.0, scalar2=None, op0=ALU.mult)
             else:
-                nc.vector.tensor_copy(out=whole[j][:], in_=turns[j][:])
+                nc.vector.tensor_copy(out=whole[q][:], in_=turns[q][:])
 
-        def fraction(j):
-            if two_transposes(j):
-                minus[j] = nega.tile([P, NB], F32, name="minus")
-                nc.vector.tensor_copy(out=minus[j][:], in_=whole[j][:])
+        def fraction(q):
+            if two_transposes(q):
+                minus[q] = nega.tile([P, 2, NB], F32, name="minus")
+                nc.vector.tensor_copy(out=minus[q][:], in_=whole[q][:])
             else:
-                nc.vector.tensor_tensor(out=turns[j][:], in0=turns[j][:], in1=whole[j][:], op=ALU.subtract)
+                nc.vector.tensor_tensor(out=turns[q][:], in0=turns[q][:], in1=whole[q][:], op=ALU.subtract)
 
         def turn_back(j):
+            q, k = divmod(j, 2)
             back[j] = psum_b.tile([P, NB], F32, name="back", tag="tr")
             for s in range(4):
                 blk = slice(s * P, (s + 1) * P)
-                if two_transposes(j):
-                    nc.tensor.matmul(out=back[j][:, blk], lhsT=turns[j][:, blk], rhs=ident_f[:], is_transpose=True,
+                if two_transposes(q):
+                    nc.tensor.matmul(out=back[j][:, blk], lhsT=turns[q][:, k, blk], rhs=ident_f[:], is_transpose=True,
                                      start=True, stop=False)
-                    nc.tensor.matmul(out=back[j][:, blk], lhsT=minus[j][:, blk], rhs=ident_f[:], is_transpose=True,
+                    nc.tensor.matmul(out=back[j][:, blk], lhsT=minus[q][:, k, blk], rhs=ident_f[:], is_transpose=True,
                                      start=False, stop=True)
                 else:
-                    nc.tensor.transpose(back[j][:, blk], turns[j][:, blk], ident_f[:])
+                    nc.tensor.transpose(back[j][:, blk], turns[q][:, k, blk], ident_f[:])
 
         def sine(j):
             u, m = divmod(j, 4)
@@ -213,27 +216,36 @@ def tile_rff_kernel(tc, lt_weight, Lambdas, bias, out):
             nc.vector.tensor_scalar(out=res[u][:], in0=res[u][:], scalar1=0.0625, scalar2=None, op0=ALU.mult)
             nc.sync.dma_start(out=out_view[:, 4 * c:4 * c + 4, jq * NB:(jq + 1) * NB], in_=res[u][:])
 
-        def pair(s):
-            return [j for j in (2 * s, 2 * s + 1) if 0 <= j < NBANK]
+        def finish_half(u, h):
+            c, jq = divmod(u, NCH)
+            lo = h * (NB // 2)
+            part = res[u][:, :, lo:lo + NB // 2]
+            nc.vector.tensor_scalar(out=part, in0=part, scalar1=0.0625, scalar2=None, op0=ALU.mult)
+            nc.sync.dma_start(out=out_view[:, 4 * c:4 * c + 4, jq * NB + lo:jq * NB + lo + NB // 2], in_=part)
+
+        def banks(q):
+            return [j for j in (2 * q, 2 * q + 1) if 0 <= j < NBANK]
 
         with tc.manual_schedule():
-            for s in range(NPAIR + 6 + 1):
-                for j in pair(s):
+            for s in range(NPAIR + 8):
+                for j in banks(s):
                     product(j)
-                for j in pair(s - 3):
+                for j in banks(s - 4):
                     turn_back(j)
                 for k in range(2):
-                    for j in pair(s - 1)[k:k + 1]:
+                    for j in banks(s - 1)[k:k + 1]:
                         if not on_vector(j):
                             leave(j)
-                    for j in pair(s - 4)[k:k + 1]:
+                    for j in banks(s - 5)[k:k + 1]:
                         sine(j)
-                for j in pair(s - 2):
-                    whole_turns(j)
-                for j in pair(s - 1):
+                if 0 <= s - 2 < NPAIR:
+                    whole_turns(s - 2)
+                for j in banks(s - 1):
                     if on_vector(j):
                         leave(j)
-                if (s - 6) % 2 == 0 and 0 <= (s - 6) // 2 < NBANK // 4:
-                    finish((s - 6) // 2)
-                for j in pair(s - 2):
-                    fraction(j)
+                if 0 <= s - 3 < NPAIR:
+                    fraction(s - 3)
+                if (s - 7) % 2 == 0 and 0 <= (s - 7) // 2 < NBANK // 4 - 1:
+                    finish((s - 7) // 2)
+                if s - 6 in (NPAIR - 2, NPAIR - 1):
+                    finish_half(NBANK // 4 - 1, s - 6 - (NPAIR - 2))

@@ -29,11 +29,11 @@ NPAIR = NBANK // 2
 
 
 def on_vector(j):
-    return j % 7 == 5
+    return j % 4 == 1
 
 
 def two_transposes(q):
-    return q % 2 == 1
+    return True
 
 
 def tile_rff_kernel(tc, lt_weight, Lambdas, bias, out):

@@ -14,26 +14,28 @@ ALU = mybir.AluOpType
 ACT = mybir.ActivationFunctionType
 
 SIZE, DIM, FDIM = 3072, 512, 2048
-P = 128
-PACK = 4
-NT = SIZE // P
-NB = 512
-NCH = FDIM // NB
 EPS = 1e-5
 TWO_PI = 2.0 * math.pi
+FACTOR = math.sqrt(2.0 / DIM)
 FLOPS = 2 * SIZE * DIM * FDIM
 
-
-NBANK = (SIZE // NB) * (FDIM // P)
+P = 128
+PACK = 4
+NB = 512
+NT = SIZE // P
+NCHUNK = SIZE // NB
+NFB = FDIM // P
+NQUARTER = FDIM // NB
+NBANK = NCHUNK * NFB
 NPAIR = NBANK // 2
+PAIRS_PER_CHUNK = NFB // 2
+
+LEAVE, WHOLE, FRACTION, TURN, SINE, FINISH = 1, 2, 3, 4, 5, 6
+AHEAD = 4
 
 
-def on_vector(j):
-    return j % 4 == 1
-
-
-def two_transposes(q):
-    return True
+def tensor_subtracts(q):
+    return q % 2 == 1
 
 
 def tile_rff_kernel(tc, lt_weight, Lambdas, bias, out):
@@ -45,12 +47,13 @@ def tile_rff_kernel(tc, lt_weight, Lambdas, bias, out):
     with ExitStack() as ctx:
         keep = ctx.enter_context(tc.tile_pool(name="keep", bufs=1))
         stage = ctx.enter_context(tc.tile_pool(name="stage", bufs=2))
-        work = ctx.enter_context(tc.tile_pool(name="work", bufs=4))
         bank = ctx.enter_context(tc.tile_pool(name="bank", bufs=6))
-        nega = ctx.enter_context(tc.tile_pool(name="nega", bufs=3))
         ints = ctx.enter_context(tc.tile_pool(name="ints", bufs=3))
-        psum_a = ctx.enter_context(tc.psum_pool(name="psum_a", bufs=4))
-        psum_b = ctx.enter_context(tc.psum_pool(name="psum_b", bufs=4))
+        nega = ctx.enter_context(tc.tile_pool(name="nega", bufs=3))
+        work = ctx.enter_context(tc.tile_pool(name="work", bufs=4))
+        psum_m = ctx.enter_context(tc.psum_pool(name="psum_m", bufs=4))
+        psum_t = ctx.enter_context(tc.psum_pool(name="psum_t", bufs=4))
+        ctx.enter_context(tc.manual_schedule())
 
         x_sb = keep.tile([P, NT, DIM], BF16)
         e_sb = keep.tile([P, NT, DIM], BF16)
@@ -61,7 +64,7 @@ def tile_rff_kernel(tc, lt_weight, Lambdas, bias, out):
         e_codes = keep.tile([P, SIZE], U32, align_bytes=64)
         e_scales = keep.tile([P, SIZE], U8, align_bytes=64)
         bias_rows = keep.tile([P, P], BF16)
-        phase = keep.tile([P, FDIM // P], F32)
+        phase = keep.tile([P, NFB], F32)
         ident = keep.tile([P, P], BF16)
         ident_f = keep.tile([P, P], F32)
         warm = keep.tile([P, 1], F32)
@@ -71,77 +74,67 @@ def tile_rff_kernel(tc, lt_weight, Lambdas, bias, out):
         rcp = keep.tile([P, NT], F32)
         fac = keep.tile([P, NT], F32)
 
-        half = FDIM // 2
-        nc.vector.memset(bias_rows[:], 0.0)
-        nc.sync.dma_start(out=x_sb[:, 0:4, :], in_=x_view[:, 0:4, :])
-        nc.sync.dma_start(out=lam_raw[:, :, 0:half], in_=lam_view[:, :, 0:half])
-        nc.sync.dma_start(out=x_sb[:, 4:8, :], in_=x_view[:, 4:8, :])
-        nc.sync.dma_start(out=lam_raw[:, :, half:FDIM], in_=lam_view[:, :, half:FDIM])
-        nc.sync.dma_start(out=bias_rows[0:FDIM // P, :], in_=bias.rearrange("(a b) -> a b", b=P))
-        for g in (8, 12, 16, 20):
-            nc.sync.dma_start(out=x_sb[:, g:g + 4, :], in_=x_view[:, g:g + 4, :])
 
-        nc.vector.memset(warm[:], 1.0)
-        nc.scalar.activation(out=warm[:], in_=warm[:], func=ACT.Sqrt)
-        make_identity(nc, ident[:])
-        make_identity(nc, ident_f[:])
+        def load_x(c):
+            nc.sync.dma_start(out=x_sb[:, 4 * c:4 * c + 4, :], in_=x_view[:, 4 * c:4 * c + 4, :])
 
-        def clip_factor(lo, hi):
-            for n in range(lo, hi):
+        def load_lam(v):
+            cols = slice(v * NB, (v + 1) * NB)
+            nc.sync.dma_start(out=lam_raw[:, :, cols], in_=lam_view[:, :, cols])
+
+        def squares(c):
+            for n in range(4 * c, 4 * c + 4):
                 junk = stage.tile([P, DIM], BF16)
                 nc.scalar.activation(out=junk[:], in_=x_sb[:, n, :], func=ACT.Square, accum_out=n2[:, n:n + 1])
-            nc.scalar.activation(out=nrm[:, lo:hi], in_=n2[:, lo:hi], func=ACT.Sqrt)
-            nc.vector.tensor_scalar_max(out=floor[:, lo:hi], in0=nrm[:, lo:hi], scalar1=EPS)
-            nc.vector.reciprocal(out=rcp[:, lo:hi], in_=floor[:, lo:hi])
-            nc.vector.tensor_scalar(out=fac[:, lo:hi], in0=rcp[:, lo:hi], scalar1=1.0 - EPS, scalar2=1.0,
-                                    op0=ALU.mult, op1=ALU.min)
 
-        def front(q):
-            grouped = stage.tile([P, 4, P, PACK], BF16, align_bytes=64)
-            for h in range(2):
-                xt = psum_a.tile([P, 2, PACK, P], BF16, tag="mm")
-                for m in range(2):
-                    n = 4 * q + 2 * h + m
-                    nc.vector.tensor_scalar(out=e_sb[:, n, :], in0=x_sb[:, n, :], scalar1=fac[:, n:n + 1],
-                                            scalar2=None, op0=ALU.mult)
-                    for t in range(PACK):
-                        nc.tensor.transpose(xt[:, m, t, :], e_sb[:, n, t * P:(t + 1) * P], ident[:])
-                if h == 0:
-                    nc.scalar.copy(out=grouped[:, 2 * h:2 * h + 2, :, :], in_=xt[:].rearrange("p m t r -> p m r t"))
-                else:
-                    nc.vector.tensor_copy(out=grouped[:, 2 * h:2 * h + 2, :, :],
-                                          in_=xt[:].rearrange("p m t r -> p m r t"))
-            cols = slice(q * NB, (q + 1) * NB)
-            nc.vector.quantize_mx(
-                out=e_codes[:, cols].bitcast(FP8X4),
-                scales=e_scales[:, cols],
-                in_=grouped[:].rearrange("p m r t -> p (m r t)"),
-            )
+        def root(first, last):
+            nc.scalar.activation(out=nrm[:, first:last], in_=n2[:, first:last], func=ACT.Sqrt)
 
-        for q in range(SIZE // NB):
-            clip_factor(4 * q, 4 * q + 4)
+        def clip_factor(first, last, link):
+            tiles = slice(first, last)
+            if link == 0:
+                nc.vector.tensor_scalar_max(out=floor[:, tiles], in0=nrm[:, tiles], scalar1=EPS)
+            elif link == 1:
+                nc.vector.reciprocal(out=rcp[:, tiles], in_=floor[:, tiles])
+            else:
+                nc.vector.tensor_scalar(out=fac[:, tiles], in0=rcp[:, tiles], scalar1=1.0 - EPS, scalar2=1.0,
+                                        op0=ALU.mult, op1=ALU.min)
 
-        for c in range(NCH):
+        def clip(n):
+            nc.vector.tensor_scalar(out=e_sb[:, n, :], in0=x_sb[:, n, :], scalar1=fac[:, n:n + 1], scalar2=None,
+                                    op0=ALU.mult)
+
+        flipped = {}
+        grouped = {}
+
+        def flip(c, h):
+            flipped[c, h] = psum_m.tile([P, 2, PACK, P], BF16, name="flipped", tag="acc")
+            for d in range(2):
+                n = 4 * c + 2 * h + d
+                for t in range(PACK):
+                    nc.tensor.transpose(flipped[c, h][:, d, t, :], e_sb[:, n, t * P:(t + 1) * P], ident[:])
+
+        def gather(c, h):
+            if h == 0:
+                grouped[c] = stage.tile([P, 4, P, PACK], BF16, name="grouped", align_bytes=64)
+            nc.vector.tensor_copy(out=grouped[c][:, 2 * h:2 * h + 2, :, :],
+                                  in_=flipped[c, h][:].rearrange("p d t r -> p d r t"))
+
+        def quantise_e(c):
             cols = slice(c * NB, (c + 1) * NB)
-            nc.vector.tensor_copy(
-                out=lam_g[:, cols, :].rearrange("p (c i) t -> p c t i", i=4),
-                in_=lam_raw[:, :, cols].rearrange("p t (c i) -> p c t i", i=4),
-            )
-        for c in range(NCH):
-            cols = slice(c * NB, (c + 1) * NB)
-            nc.vector.quantize_mx(
-                out=lam_codes[:, cols].bitcast(FP8X4),
-                scales=lam_scales[:, cols],
-                in_=lam_g[:, cols, :].rearrange("p c t -> p (c t)"),
-            )
+            nc.vector.quantize_mx(out=e_codes[:, cols].bitcast(FP8X4), scales=e_scales[:, cols],
+                                  in_=grouped[c][:].rearrange("p a r t -> p (a r t)"))
 
-        bias_t = psum_b.tile([P, P], BF16, tag="tr")
-        nc.tensor.transpose(bias_t[:], bias_rows[:], ident[:])
-        nc.vector.tensor_scalar(out=phase[:], in0=bias_t[:, 0:FDIM // P], scalar1=0.5 * math.pi, scalar2=1.0 / TWO_PI,
-                                op0=ALU.add, op1=ALU.mult)
+        def regroup_lam(v):
+            cols = slice(v * NB, (v + 1) * NB)
+            nc.vector.tensor_copy(out=lam_g[:, cols, :].rearrange("p (y w) t -> p y t w", w=4),
+                                  in_=lam_raw[:, :, cols].rearrange("p t (y w) -> p y t w", w=4))
 
-        for q in range(SIZE // NB):
-            front(q)
+        def quantise_lam(v):
+            cols = slice(v * NB, (v + 1) * NB)
+            nc.vector.quantize_mx(out=lam_codes[:, cols].bitcast(FP8X4), scales=lam_scales[:, cols],
+                                  in_=lam_g[:, cols, :].rearrange("p f t -> p (f t)"))
+
 
         acc = {}
         turns = {}
@@ -151,101 +144,164 @@ def tile_rff_kernel(tc, lt_weight, Lambdas, bias, out):
         res = {}
 
         def product(j):
-            c, jb = divmod(j, FDIM // P)
-            fcols = slice(jb * P, (jb + 1) * P)
-            ecols = slice(c * NB, (c + 1) * NB)
-            acc[j] = psum_a.tile([P, NB], F32, name="acc", tag="mm")
-            nc.tensor.matmul_mx(
-                out=acc[j][:],
-                lhsT=lam_codes[:, fcols].bitcast(FP8X4),
-                lhsT_scale=lam_scales[:, fcols],
-                rhs=e_codes[:, ecols].bitcast(FP8X4),
-                rhs_scale=e_scales[:, ecols],
-                start=True,
-                stop=True,
-            )
+            c, fb = divmod(j, NFB)
+            feats = slice(fb * P, (fb + 1) * P)
+            rows = slice(c * NB, (c + 1) * NB)
+            acc[j] = psum_m.tile([P, NB], F32, name="acc")
+            nc.tensor.matmul_mx(out=acc[j][:], lhsT=lam_codes[:, feats].bitcast(FP8X4), lhsT_scale=lam_scales[:, feats],
+                                rhs=e_codes[:, rows].bitcast(FP8X4), rhs_scale=e_scales[:, rows], start=True, stop=True)
 
         def leave(j):
-            jb = j % (FDIM // P)
-            q, k = divmod(j, 2)
-            if q not in turns:
+            q, odd = divmod(j, 2)
+            fb = j % NFB
+            if odd == 0:
                 turns[q] = bank.tile([P, 2, NB], F32, name="turns")
-            if on_vector(j):
-                nc.vector.tensor_scalar(out=turns[q][:, k, :], in0=acc[j][:], scalar1=1.0 / TWO_PI,
-                                        scalar2=phase[:, jb:jb + 1], op0=ALU.mult, op1=ALU.add)
-            else:
-                nc.scalar.activation(out=turns[q][:, k, :], in_=acc[j][:], func=ACT.Identity, scale=1.0 / TWO_PI,
-                                     bias=phase[:, jb:jb + 1])
+            nc.scalar.activation(out=turns[q][:, odd, :], in_=acc[j][:], func=ACT.Identity, scale=1.0 / TWO_PI,
+                                 bias=phase[:, fb:fb + 1])
 
         def whole_turns(q):
             whole[q] = ints.tile([P, 2, NB], I32, name="whole")
-            if two_transposes(q):
+            if tensor_subtracts(q):
                 nc.vector.tensor_scalar(out=whole[q][:], in0=turns[q][:], scalar1=-1.0, scalar2=None, op0=ALU.mult)
             else:
                 nc.vector.tensor_copy(out=whole[q][:], in_=turns[q][:])
 
         def fraction(q):
-            if two_transposes(q):
+            if tensor_subtracts(q):
                 minus[q] = nega.tile([P, 2, NB], F32, name="minus")
                 nc.vector.tensor_copy(out=minus[q][:], in_=whole[q][:])
             else:
                 nc.vector.tensor_tensor(out=turns[q][:], in0=turns[q][:], in1=whole[q][:], op=ALU.subtract)
 
         def turn_back(j):
-            q, k = divmod(j, 2)
-            back[j] = psum_b.tile([P, NB], F32, name="back", tag="tr")
-            for s in range(4):
-                blk = slice(s * P, (s + 1) * P)
-                if two_transposes(q):
-                    nc.tensor.matmul(out=back[j][:, blk], lhsT=turns[q][:, k, blk], rhs=ident_f[:], is_transpose=True,
+            q, odd = divmod(j, 2)
+            back[j] = psum_t.tile([P, NB], F32, name="back")
+            for a in range(4):
+                blk = slice(a * P, (a + 1) * P)
+                if tensor_subtracts(q):
+                    nc.tensor.matmul(out=back[j][:, blk], lhsT=turns[q][:, odd, blk], rhs=ident_f[:], is_transpose=True,
                                      start=True, stop=False)
-                    nc.tensor.matmul(out=back[j][:, blk], lhsT=minus[q][:, k, blk], rhs=ident_f[:], is_transpose=True,
+                    nc.tensor.matmul(out=back[j][:, blk], lhsT=minus[q][:, odd, blk], rhs=ident_f[:], is_transpose=True,
                                      start=False, stop=True)
                 else:
-                    nc.tensor.transpose(back[j][:, blk], turns[q][:, k, blk], ident_f[:])
+                    nc.tensor.transpose(back[j][:, blk], turns[q][:, odd, blk], ident_f[:])
 
         def sine(j):
-            u, m = divmod(j, 4)
-            if m == 0:
+            u, b = divmod(j, 4)
+            if b == 0:
                 res[u] = work.tile([P, 4, NB], F32, name="res")
-            nc.scalar.activation(out=res[u][:, :, m * P:(m + 1) * P], in_=back[j][:].rearrange("p (s j) -> p s j", s=4),
+            nc.scalar.activation(out=res[u][:, :, b * P:(b + 1) * P], in_=back[j][:].rearrange("p (a f) -> p a f", a=4),
                                  func=ACT.Sin, scale=TWO_PI)
 
-        def finish(u):
-            c, jq = divmod(u, NCH)
-            nc.vector.tensor_scalar(out=res[u][:], in0=res[u][:], scalar1=0.0625, scalar2=None, op0=ALU.mult)
-            nc.sync.dma_start(out=out_view[:, 4 * c:4 * c + 4, jq * NB:(jq + 1) * NB], in_=res[u][:])
-
-        def finish_half(u, h):
-            c, jq = divmod(u, NCH)
-            lo = h * (NB // 2)
-            part = res[u][:, :, lo:lo + NB // 2]
-            nc.vector.tensor_scalar(out=part, in0=part, scalar1=0.0625, scalar2=None, op0=ALU.mult)
-            nc.sync.dma_start(out=out_view[:, 4 * c:4 * c + 4, jq * NB + lo:jq * NB + lo + NB // 2], in_=part)
+        def finish(q):
+            u, side = divmod(q, 2)
+            c, v = divmod(u, NQUARTER)
+            left = side * 2 * P
+            piece = res[u][:, :, left:left + 2 * P]
+            nc.vector.tensor_scalar(out=piece, in0=piece, scalar1=FACTOR, scalar2=None, op0=ALU.mult)
+            nc.sync.dma_start(out=out_view[:, 4 * c:4 * c + 4, v * NB + left:v * NB + left + 2 * P], in_=piece)
 
         def banks(q):
-            return [j for j in (2 * q, 2 * q + 1) if 0 <= j < NBANK]
+            return [j for j in (2 * q, 2 * q + 1) if 0 <= q < NPAIR]
 
-        with tc.manual_schedule():
-            for s in range(NPAIR + 8):
+        def pairs(q):
+            return [q] if 0 <= q < NPAIR else []
+
+
+        nc.vector.memset(bias_rows[:], 0.0)
+        nc.vector.memset(warm[:], 1.0)
+        load_x(0)
+        nc.sync.dma_start(out=bias_rows[0:NFB, :], in_=bias.rearrange("(fb f) -> fb f", f=P))
+        load_lam(0)
+        load_x(1)
+        load_lam(1)
+        load_x(2)
+        load_lam(2)
+        load_lam(3)
+        load_x(3)
+        load_x(4)
+        load_x(5)
+
+        nc.scalar.activation(out=warm[:], in_=warm[:], func=ACT.Sqrt)
+        make_identity(nc, ident[:])
+        make_identity(nc, ident_f[:])
+
+        squares(0)
+        root(0, 4)
+        squares(1)
+        root(4, 8)
+        for c in range(2, NCHUNK):
+            squares(c)
+        root(8, NT)
+
+        bias_t = psum_t.tile([P, P], BF16, name="bias_t", tag="back")
+        nc.tensor.transpose(bias_t[:], bias_rows[:], ident[:])
+        nc.vector.tensor_scalar(out=phase[:], in0=bias_t[:, 0:NFB], scalar1=0.5 * math.pi, scalar2=1.0 / TWO_PI,
+                                op0=ALU.add, op1=ALU.mult)
+
+        regroup_lam(0)
+        for link in range(3):
+            clip_factor(0, 4, link)
+        for n in range(0, 4):
+            clip(n)
+        flip(0, 0)
+        flip(0, 1)
+        regroup_lam(1)
+        gather(0, 0)
+        regroup_lam(2)
+        gather(0, 1)
+        quantise_lam(0)
+        clip_factor(4, 8, 0)
+        regroup_lam(3)
+        clip_factor(4, 8, 1)
+        quantise_e(0)
+        clip_factor(4, 8, 2)
+        quantise_lam(1)
+        for n in range(4, 8):
+            clip(n)
+        flip(1, 0)
+        flip(1, 1)
+        quantise_lam(2)
+        quantise_lam(3)
+        gather(1, 0)
+        gather(1, 1)
+        for j in banks(0):
+            product(j)
+        clip_factor(8, NT, 0)
+        quantise_e(1)
+        clip_factor(8, NT, 1)
+
+
+        for s in range(NPAIR + FINISH + 1):
+            c_front, part = divmod(s + AHEAD, PAIRS_PER_CHUNK)
+            c_front += 1
+            if not 2 <= c_front < NCHUNK:
+                part = -1
+
+            for j in banks(s - LEAVE):
+                leave(j)
+            if s > 0:
                 for j in banks(s):
                     product(j)
-                for j in banks(s - 4):
-                    turn_back(j)
-                for k in range(2):
-                    for j in banks(s - 1)[k:k + 1]:
-                        if not on_vector(j):
-                            leave(j)
-                    for j in banks(s - 5)[k:k + 1]:
-                        sine(j)
-                if 0 <= s - 2 < NPAIR:
-                    whole_turns(s - 2)
-                for j in banks(s - 1):
-                    if on_vector(j):
-                        leave(j)
-                if 0 <= s - 3 < NPAIR:
-                    fraction(s - 3)
-                if (s - 7) % 2 == 0 and 0 <= (s - 7) // 2 < NBANK // 4 - 1:
-                    finish((s - 7) // 2)
-                if s - 6 in (NPAIR - 2, NPAIR - 1):
-                    finish_half(NBANK // 4 - 1, s - 6 - (NPAIR - 2))
+            for j in banks(s - TURN):
+                turn_back(j)
+            if part in (2, 4):
+                flip(c_front, part // 2 - 1)
+            for j in banks(s - SINE):
+                sine(j)
+
+            for q in pairs(s - WHOLE):
+                whole_turns(q)
+            if s == 1:
+                clip_factor(8, NT, 2)
+            if part in (0, 1):
+                clip(4 * c_front + 2 * part)
+                clip(4 * c_front + 2 * part + 1)
+            if part in (3, 5):
+                gather(c_front, part // 2 - 1)
+            if part == 7:
+                quantise_e(c_front)
+            for q in pairs(s - FRACTION):
+                fraction(q)
+            for q in pairs(s - FINISH):
+                finish(q)

import math
from contextlib import ExitStack

import concourse.mybir as mybir
from concourse.masks import make_identity

F32 = mybir.dt.float32
BF16 = mybir.dt.bfloat16
I32 = mybir.dt.int32
U32 = mybir.dt.uint32
U8 = mybir.dt.uint8
FP8X4 = mybir.dt.float8_e4m3fn_x4
ALU = mybir.AluOpType
ACT = mybir.ActivationFunctionType

SIZE, DIM, FDIM = 3072, 512, 2048
EPS = 1e-5
TWO_PI = 2.0 * math.pi
FACTOR = math.sqrt(2.0 / DIM)
FLOPS = 2 * SIZE * DIM * FDIM

P = 128
PACK = 4
NB = 512
NT = SIZE // P
NCHUNK = SIZE // NB
NFB = FDIM // P
NQUARTER = FDIM // NB
NBANK = NCHUNK * NFB
NPAIR = NBANK // 2
PAIRS_PER_CHUNK = NFB // 2

LEAVE, WHOLE, FRACTION, TURN, SINE, FINISH = 1, 2, 3, 4, 5, 6
AHEAD = 4


def tensor_subtracts(q):
    return q % 2 == 1


def tile_rff_kernel(tc, lt_weight, Lambdas, bias, out):
    nc = tc.nc
    x_view = lt_weight.rearrange("(p n) k -> p n k", n=NT)
    out_view = out.rearrange("(p n) f -> p n f", n=NT)
    lam_view = Lambdas.rearrange("(t p) f -> p t f", p=P)

    with ExitStack() as ctx:
        keep = ctx.enter_context(tc.tile_pool(name="keep", bufs=1))
        stage = ctx.enter_context(tc.tile_pool(name="stage", bufs=2))
        bank = ctx.enter_context(tc.tile_pool(name="bank", bufs=6))
        ints = ctx.enter_context(tc.tile_pool(name="ints", bufs=3))
        nega = ctx.enter_context(tc.tile_pool(name="nega", bufs=3))
        work = ctx.enter_context(tc.tile_pool(name="work", bufs=4))
        psum_m = ctx.enter_context(tc.psum_pool(name="psum_m", bufs=4))
        psum_t = ctx.enter_context(tc.psum_pool(name="psum_t", bufs=4))
        ctx.enter_context(tc.manual_schedule())

        x_sb = keep.tile([P, NT, DIM], BF16)
        e_sb = keep.tile([P, NT, DIM], BF16)
        lam_raw = keep.tile([P, PACK, FDIM], BF16)
        lam_g = keep.tile([P, FDIM, PACK], BF16, align_bytes=64)
        lam_codes = keep.tile([P, FDIM], U32, align_bytes=64)
        lam_scales = keep.tile([P, FDIM], U8, align_bytes=64)
        e_codes = keep.tile([P, SIZE], U32, align_bytes=64)
        e_scales = keep.tile([P, SIZE], U8, align_bytes=64)
        bias_rows = keep.tile([P, P], BF16)
        phase = keep.tile([P, NFB], F32)
        ident = keep.tile([P, P], BF16)
        ident_f = keep.tile([P, P], F32)
        warm = keep.tile([P, 1], F32)
        n2 = keep.tile([P, NT], F32)
        nrm = keep.tile([P, NT], F32)
        floor = keep.tile([P, NT], F32)
        rcp = keep.tile([P, NT], F32)
        fac = keep.tile([P, NT], F32)


        def load_x(c):
            nc.sync.dma_start(out=x_sb[:, 4 * c:4 * c + 4, :], in_=x_view[:, 4 * c:4 * c + 4, :])

        def load_lam(v):
            cols = slice(v * NB, (v + 1) * NB)
            nc.sync.dma_start(out=lam_raw[:, :, cols], in_=lam_view[:, :, cols])

        def squares(c):
            for n in range(4 * c, 4 * c + 4):
                junk = stage.tile([P, DIM], BF16)
                nc.scalar.activation(out=junk[:], in_=x_sb[:, n, :], func=ACT.Square, accum_out=n2[:, n:n + 1])

        def root(first, last):
            nc.scalar.activation(out=nrm[:, first:last], in_=n2[:, first:last], func=ACT.Sqrt)

        def clip_factor(first, last, link):
            tiles = slice(first, last)
            if link == 0:
                nc.vector.tensor_scalar_max(out=floor[:, tiles], in0=nrm[:, tiles], scalar1=EPS)
            elif link == 1:
                nc.vector.reciprocal(out=rcp[:, tiles], in_=floor[:, tiles])
            else:
                nc.vector.tensor_scalar(out=fac[:, tiles], in0=rcp[:, tiles], scalar1=1.0 - EPS, scalar2=1.0,
                                        op0=ALU.mult, op1=ALU.min)

        def clip(n):
            nc.vector.tensor_scalar(out=e_sb[:, n, :], in0=x_sb[:, n, :], scalar1=fac[:, n:n + 1], scalar2=None,
                                    op0=ALU.mult)

        flipped = {}
        grouped = {}

        def flip(c, h):
            flipped[c, h] = psum_m.tile([P, 2, PACK, P], BF16, name="flipped", tag="acc")
            for d in range(2):
                n = 4 * c + 2 * h + d
                for t in range(PACK):
                    nc.tensor.transpose(flipped[c, h][:, d, t, :], e_sb[:, n, t * P:(t + 1) * P], ident[:])

        def gather(c, h):
            if h == 0:
                grouped[c] = stage.tile([P, 4, P, PACK], BF16, name="grouped", align_bytes=64)
            nc.vector.tensor_copy(out=grouped[c][:, 2 * h:2 * h + 2, :, :],
                                  in_=flipped[c, h][:].rearrange("p d t r -> p d r t"))

        def quantise_e(c):
            cols = slice(c * NB, (c + 1) * NB)
            nc.vector.quantize_mx(out=e_codes[:, cols].bitcast(FP8X4), scales=e_scales[:, cols],
                                  in_=grouped[c][:].rearrange("p a r t -> p (a r t)"))

        def regroup_lam(v):
            cols = slice(v * NB, (v + 1) * NB)
            nc.vector.tensor_copy(out=lam_g[:, cols, :].rearrange("p (y w) t -> p y t w", w=4),
                                  in_=lam_raw[:, :, cols].rearrange("p t (y w) -> p y t w", w=4))

        def quantise_lam(v):
            cols = slice(v * NB, (v + 1) * NB)
            nc.vector.quantize_mx(out=lam_codes[:, cols].bitcast(FP8X4), scales=lam_scales[:, cols],
                                  in_=lam_g[:, cols, :].rearrange("p f t -> p (f t)"))


        acc = {}
        turns = {}
        whole = {}
        minus = {}
        back = {}
        res = {}

        def product(j):
            c, fb = divmod(j, NFB)
            feats = slice(fb * P, (fb + 1) * P)
            rows = slice(c * NB, (c + 1) * NB)
            acc[j] = psum_m.tile([P, NB], F32, name="acc")
            nc.tensor.matmul_mx(out=acc[j][:], lhsT=lam_codes[:, feats].bitcast(FP8X4), lhsT_scale=lam_scales[:, feats],
                                rhs=e_codes[:, rows].bitcast(FP8X4), rhs_scale=e_scales[:, rows], start=True, stop=True)

        def leave(j):
            q, odd = divmod(j, 2)
            fb = j % NFB
            if odd == 0:
                turns[q] = bank.tile([P, 2, NB], F32, name="turns")
            nc.scalar.activation(out=turns[q][:, odd, :], in_=acc[j][:], func=ACT.Identity, scale=1.0 / TWO_PI,
                                 bias=phase[:, fb:fb + 1])

        def whole_turns(q):
            whole[q] = ints.tile([P, 2, NB], I32, name="whole")
            if tensor_subtracts(q):
                nc.vector.tensor_scalar(out=whole[q][:], in0=turns[q][:], scalar1=-1.0, scalar2=None, op0=ALU.mult)
            else:
                nc.vector.tensor_copy(out=whole[q][:], in_=turns[q][:])

        def fraction(q):
            if tensor_subtracts(q):
                minus[q] = nega.tile([P, 2, NB], F32, name="minus")
                nc.vector.tensor_copy(out=minus[q][:], in_=whole[q][:])
            else:
                nc.vector.tensor_tensor(out=turns[q][:], in0=turns[q][:], in1=whole[q][:], op=ALU.subtract)

        def turn_back(j):
            q, odd = divmod(j, 2)
            back[j] = psum_t.tile([P, NB], F32, name="back")
            for a in range(4):
                blk = slice(a * P, (a + 1) * P)
                if tensor_subtracts(q):
                    nc.tensor.matmul(out=back[j][:, blk], lhsT=turns[q][:, odd, blk], rhs=ident_f[:], is_transpose=True,
                                     start=True, stop=False)
                    nc.tensor.matmul(out=back[j][:, blk], lhsT=minus[q][:, odd, blk], rhs=ident_f[:], is_transpose=True,
                                     start=False, stop=True)
                else:
                    nc.tensor.transpose(back[j][:, blk], turns[q][:, odd, blk], ident_f[:])

        def sine(j):
            u, b = divmod(j, 4)
            if b == 0:
                res[u] = work.tile([P, 4, NB], F32, name="res")
            nc.scalar.activation(out=res[u][:, :, b * P:(b + 1) * P], in_=back[j][:].rearrange("p (a f) -> p a f", a=4),
                                 func=ACT.Sin, scale=TWO_PI)

        def finish(q):
            u, side = divmod(q, 2)
            c, v = divmod(u, NQUARTER)
            left = side * 2 * P
            piece = res[u][:, :, left:left + 2 * P]
            nc.vector.tensor_scalar(out=piece, in0=piece, scalar1=FACTOR, scalar2=None, op0=ALU.mult)
            nc.sync.dma_start(out=out_view[:, 4 * c:4 * c + 4, v * NB + left:v * NB + left + 2 * P], in_=piece)

        def banks(q):
            return [j for j in (2 * q, 2 * q + 1) if 0 <= q < NPAIR]

        def pairs(q):
            return [q] if 0 <= q < NPAIR else []


        nc.vector.memset(bias_rows[:], 0.0)
        nc.vector.memset(warm[:], 1.0)
        load_x(0)
        nc.sync.dma_start(out=bias_rows[0:NFB, :], in_=bias.rearrange("(fb f) -> fb f", f=P))
        load_lam(0)
        load_x(1)
        load_lam(1)
        load_x(2)
        load_lam(2)
        load_lam(3)
        load_x(3)
        load_x(4)
        load_x(5)

        nc.scalar.activation(out=warm[:], in_=warm[:], func=ACT.Sqrt)
        make_identity(nc, ident[:])
        make_identity(nc, ident_f[:])

        squares(0)
        root(0, 4)
        squares(1)
        root(4, 8)
        for c in range(2, NCHUNK):
            squares(c)
        root(8, NT)

        bias_t = psum_t.tile([P, P], BF16, name="bias_t", tag="back")
        nc.tensor.transpose(bias_t[:], bias_rows[:], ident[:])
        nc.vector.tensor_scalar(out=phase[:], in0=bias_t[:, 0:NFB], scalar1=0.5 * math.pi, scalar2=1.0 / TWO_PI,
                                op0=ALU.add, op1=ALU.mult)

        regroup_lam(0)
        for link in range(3):
            clip_factor(0, 4, link)
        for n in range(0, 4):
            clip(n)
        flip(0, 0)
        flip(0, 1)
        regroup_lam(1)
        gather(0, 0)
        regroup_lam(2)
        gather(0, 1)
        quantise_lam(0)
        clip_factor(4, 8, 0)
        regroup_lam(3)
        clip_factor(4, 8, 1)
        quantise_e(0)
        clip_factor(4, 8, 2)
        quantise_lam(1)
        for n in range(4, 8):
            clip(n)
        flip(1, 0)
        flip(1, 1)
        quantise_lam(2)
        quantise_lam(3)
        gather(1, 0)
        gather(1, 1)
        for j in banks(0):
            product(j)
        clip_factor(8, NT, 0)
        quantise_e(1)
        clip_factor(8, NT, 1)


        for s in range(NPAIR + FINISH + 1):
            c_front, part = divmod(s + AHEAD, PAIRS_PER_CHUNK)
            c_front += 1
            if not 2 <= c_front < NCHUNK:
                part = -1

            for j in banks(s - LEAVE):
                leave(j)
            if s > 0:
                for j in banks(s):
                    product(j)
            for j in banks(s - TURN):
                turn_back(j)
            if part in (2, 4):
                flip(c_front, part // 2 - 1)
            for j in banks(s - SINE):
                sine(j)

            for q in pairs(s - WHOLE):
                whole_turns(q)
            if s == 1:
                clip_factor(8, NT, 2)
            if part in (0, 1):
                clip(4 * c_front + 2 * part)
                clip(4 * c_front + 2 * part + 1)
            if part in (3, 5):
                gather(c_front, part // 2 - 1)
            if part == 7:
                quantise_e(c_front)
            for q in pairs(s - FRACTION):
                fraction(q)
            for q in pairs(s - FINISH):
                finish(q)
